import numpy as np
import ml_dtypes


def mxq(x, axis, fmt="e4m3"):
    dtype, down = {"e4m3": (ml_dtypes.float8_e4m3fn, 7), "e5m2": (ml_dtypes.float8_e5m2, 14)}[fmt]
    v = np.moveaxis(np.asarray(x, np.float32).astype(ml_dtypes.bfloat16).astype(np.float64), axis, -1)
    blocks = v.reshape(v.shape[:-1] + (-1, 32))
    amax = np.abs(blocks).max(-1, keepdims=True)
    byte = np.maximum(np.where(amax > 0, np.frexp(amax)[1] - 1 + 127, 0) - down, 1)
    scale = np.exp2(byte - 127.0)
    codes = (blocks / scale).astype(np.float32).astype(dtype).astype(np.float64)
    return np.moveaxis((codes * scale).reshape(v.shape), -1, axis)


WIDE = False


def mx_kscale(k):
    if not WIDE:
        return np.ones(k)
    levels = np.array([10, -10, 5, -5, 0])
    a = np.random.permutation(np.resize(levels, k // 512 * 4)).reshape(k // 512, 4)
    idx = np.arange(k)
    return np.exp2(a[idx // 512, idx % 128 // 32])


BF16 = ml_dtypes.bfloat16


def bf(x):
    return np.asarray(x, np.float32).astype(BF16)


def f64(x):
    return np.asarray(x).astype(np.float64)


E2M1 = np.array([0.0, 0.5, 1.0, 1.5, 2.0, 3.0, 4.0, 6.0, -0.0, -0.5, -1.0, -1.5, -2.0, -3.0, -4.0, -6.0])


def pack_weight(w, fmt):
    k, n = w.shape
    w = f64(bf(w)).reshape(k // 32, 32, n)
    amax = np.abs(w).max(1)
    if fmt == "e4m3":
        byte = np.frexp(amax)[1] - 1 + 127 - 7
    else:
        mant, ex = np.frexp(amax / 6.0)
        byte = np.where(mant > 0.5, ex, ex - 1) + 127
    byte = np.clip(np.where(amax > 0, byte, 1), 1, 254)
    scaled = (w * np.exp2(127.0 - byte)[:, None, :]).reshape(k, n).astype(np.float32)
    by_word = np.ascontiguousarray(scaled.reshape(k // 512, 128, 4, n).transpose(0, 1, 3, 2))
    if fmt == "e4m3":
        words = by_word.astype(ml_dtypes.float8_e4m3fn).view(np.uint8)
    else:
        c = by_word.astype(ml_dtypes.float4_e2m1fn).view(np.uint8) & 0xF
        words = c[..., 0::2] | (c[..., 1::2] << 4)
    return np.ascontiguousarray(words), np.ascontiguousarray(byte.astype(np.uint8).reshape(k // 512, 16, n))


def unpack_weight(words, scales, fmt):
    g, p, n, _ = words.shape
    if fmt == "e4m3":
        vals = np.ascontiguousarray(words).view(ml_dtypes.float8_e4m3fn).astype(np.float64)
    else:
        nib = np.empty((g, p, n, 4), np.uint8)
        nib[..., 0::2] = words & 0xF
        nib[..., 1::2] = words >> 4
        vals = E2M1[nib]
    vals = vals * np.repeat(np.exp2(scales.astype(np.float64) - 127.0), 8, axis=1)[..., None]
    return vals.transpose(0, 1, 3, 2).reshape(g * 512, n)

def pack4(w):
    words, scales = pack_weight(w, "e2m1")
    return words.reshape(words.shape[0], 128, -1), scales


def unpack4(words, scales):
    return unpack_weight(words.reshape(words.shape[0], 128, -1, 2), scales, "e2m1")


B, I, H = 128, 2048, 1536
G = 4
MXH = H % 512 == 0


def sigmoid(v):
    return 1.0 / (1.0 + np.exp(-v))


def setup_inputs():
    s = mx_kscale(I)
    t = mx_kscale(H) if MXH else np.ones(H)
    x = bf(np.random.standard_normal((B, I)) * s)
    h = bf(np.random.standard_normal((B, H)) * t)
    c = bf(np.random.standard_normal((B, H)))
    wx = np.random.standard_normal((G, H, I)) * 0.8 / np.sqrt(I) / s
    cat = np.ascontiguousarray(wx.swapaxes(1, 2)).reshape(-1, H)
    Wx_words, Wx_scales = pack4(cat)
    Wh = bf(np.random.standard_normal((4, H, H)) * 0.8 / np.sqrt(H) / t)
    bx = bf(np.random.standard_normal((4, H)) * 0.3)
    bh = bf(np.random.standard_normal((4, H)) * 0.3)
    return {"x": x, "h": h, "c": c, "Wx_words": Wx_words, "Wx_scales": Wx_scales,
            "Wh": Wh, "bx": bx, "bh": bh}


def reference(x, h, c, Wx_words, Wx_scales, Wh, bx, bh):
    wx = unpack4(Wx_words, Wx_scales).reshape(G, I, H).swapaxes(1, 2).reshape(G * H, I)
    wh = f64(Wh).reshape(4 * H, H)
    gx = (mxq(f64(x), 1, "e4m3") @ wx.T) + f64(bx).reshape(-1)
    if MXH:
        gh = (mxq(f64(h), 1, "e4m3") @ mxq(wh, 1, "e4m3").T) + f64(bh).reshape(-1)
    else:
        gh = f64(h) @ wh.T + f64(bh).reshape(-1)
    g = (gx + gh).reshape(-1, 4, H)
    i = sigmoid(g[:, 0])
    f = sigmoid(g[:, 1])
    gc = np.tanh(g[:, 2])
    o = sigmoid(g[:, 3])
    c_new = f * f64(c) + i * gc
    hs = o * np.tanh(c_new)
    return (hs, c_new)

@@ -1,0 +1,250 @@
+from contextlib import ExitStack
+
+import concourse.mybir as mybir
+from concourse.masks import make_identity
+
+F32 = mybir.dt.float32
+BF16 = mybir.dt.bfloat16
+I32 = mybir.dt.int32
+U32 = mybir.dt.uint32
+U8 = mybir.dt.uint8
+FP8X4 = mybir.dt.float8_e4m3fn_x4
+FP4X4 = mybir.dt.float4_e2m1fn_x4
+ACT = mybir.ActivationFunctionType
+
+P = 128
+PACK = 4
+K_PASS = P * PACK
+IN = 2048
+HID = 1536
+GATES = 4
+X_PASSES = IN // K_PASS
+H_PASSES = HID // K_PASS
+PASSES = X_PASSES + H_PASSES
+N_TILE = 512
+CHUNKS = HID // N_TILE
+UNITS = GATES * CHUNKS
+WORDS_PASS = K_PASS // 2
+ROWS_PART = N_TILE // P
+LOOKAHEAD = 4
+GATE_FUNC = (ACT.Sigmoid, ACT.Sigmoid, ACT.Tanh, ACT.Sigmoid)
+
+FLOPS = 2 * P * GATES * HID * (IN + HID)
+
+
+def tile_lstmcell_w_e_kernel(tc, x, h, c, Wx_words, Wx_scales, Wh, bx, bh, out_0, out_1):
+    nc = tc.nc
+    with ExitStack() as ctx:
+        ctx.enter_context(tc.manual_schedule())
+        const = ctx.enter_context(tc.tile_pool(name="const", bufs=1))
+        raw_pool = ctx.enter_context(tc.tile_pool(name="raw", bufs=LOOKAHEAD))
+        words_pool = ctx.enter_context(tc.tile_pool(name="words", bufs=2))
+        grouped_pool = ctx.enter_context(tc.tile_pool(name="grouped", bufs=2 * H_PASSES))
+        codes_pool = ctx.enter_context(tc.tile_pool(name="codes", bufs=3))
+        transposed = ctx.enter_context(tc.psum_pool(name="transposed", bufs=5))
+        sums = ctx.enter_context(tc.psum_pool(name="sums", bufs=CHUNKS))
+
+        ident = const.tile([P, P], F32)
+        make_identity(nc, ident[:])
+        ones = const.tile([P, P], BF16)
+        nc.vector.memset(ones[:], 1.0)
+
+        x_codes = const.tile([P, X_PASSES, P], U32, align_bytes=64)
+        x_scales = const.tile([P, X_PASSES, P], U8, align_bytes=64)
+        h_codes = const.tile([P, H_PASSES, P], U32, align_bytes=64)
+        h_scales = const.tile([P, H_PASSES, P], U8, align_bytes=64)
+        wx_scales = const.tile([P, GATES * X_PASSES, HID], U8, align_bytes=64)
+        bias = const.tile([P, GATES * HID], F32)
+        c_sb = const.tile([P, HID], BF16)
+
+        raw = {}
+        wx_words = {}
+        wh_codes = {}
+
+        def load_hidden_weights(unit):
+            gate, chunk = divmod(unit, CHUNKS)
+            rows = raw_pool.tile([P, ROWS_PART, HID], BF16, tag="rows")
+            nc.sync.dma_start(
+                out=rows[:],
+                in_=Wh[gate, N_TILE * chunk : N_TILE * (chunk + 1), :].rearrange("(q r) k -> q r k", r=ROWS_PART),
+            )
+            raw[unit] = rows
+
+        def load_input_weights(gate):
+            words = words_pool.tile([P, X_PASSES, 2 * HID], U8, tag="words", align_bytes=64)
+            for s in range(X_PASSES):
+                nc.sync.dma_start(out=words[:, s, :].bitcast(I32), in_=Wx_words[X_PASSES * gate + s].bitcast(I32))
+            wx_words[gate] = words
+
+        def load_step(n):
+            if n % CHUNKS == 0 and 0 < n <= UNITS:
+                load_input_weights(n // CHUNKS - 1)
+            if n < UNITS:
+                load_hidden_weights(n)
+
+        def quantise_activation(src, passes, word_columns, grouped, codes, scales):
+            src_words = src[:].bitcast(F32)
+            for s in range(passes):
+                bank = transposed.tile([P, 2, P], F32, tag="bank")
+                for u in range(2):
+                    nc.tensor.transpose(out=bank[:, u, :], in_=src_words[:, word_columns(s, u)], identity=ident[:])
+                nc.scalar.copy(
+                    out=grouped[:, s, :].bitcast(F32).rearrange("p (b u) -> p b u", u=2),
+                    in_=bank[:].rearrange("p u b -> p b u"),
+                )
+                nc.vector.quantize_mx(out=codes[:, s, :].bitcast(FP8X4), scales=scales[:, s, :], in_=grouped[:, s, :])
+
+        with tc.tile_pool(name="head", bufs=1) as head:
+            bias_rows = head.tile([P, GATES * HID], BF16)
+            nc.vector.memset(bias_rows[:], 0.0)
+            for gate in range(GATES):
+                nc.vector.memset(wx_scales[:, X_PASSES * gate : X_PASSES * (gate + 1), :].bitcast(I32), 0)
+
+            x_raw = head.tile([P, IN], BF16)
+            nc.sync.dma_start(out=x_raw[:], in_=x[:, :])
+            h_raw = head.tile([P, HID], BF16)
+            nc.sync.dma_start(out=h_raw[:], in_=h[:, :])
+            nc.sync.dma_start(out=bias_rows[0:1, :], in_=bx.rearrange("(o g) n -> o (g n)", o=1))
+            nc.sync.dma_start(out=bias_rows[1:2, :], in_=bh.rearrange("(o g) n -> o (g n)", o=1))
+
+            for half in range(2):
+                groups = slice(8 * half, 8 * (half + 1))
+                for b in range(2):
+                    for r in range(4):
+                        nc.sync.dma_start(
+                            out=wx_scales[32 * b + r : P : 64, groups, :].bitcast(I32),
+                            in_=Wx_scales[groups, 4 * b + r : 16 : 8, :].rearrange("s q n -> q s n").bitcast(I32),
+                        )
+
+            for n in range(LOOKAHEAD):
+                load_step(n)
+            nc.sync.dma_start(out=c_sb[:], in_=c[:, :])
+
+            x_grouped = head.tile([P, X_PASSES, PACK * P], BF16, align_bytes=64)
+            quantise_activation(
+                x_raw, X_PASSES, lambda s, u: slice(WORDS_PASS * s + u, WORDS_PASS * (s + 1), 2),
+                x_grouped, x_codes, x_scales,
+            )
+            h_grouped = head.tile([P, H_PASSES, PACK * P], BF16, align_bytes=64)
+            quantise_activation(
+                h_raw, H_PASSES, lambda s, u: slice(WORDS_PASS * s + P * u, WORDS_PASS * s + P * (u + 1)),
+                h_grouped, h_codes, h_scales,
+            )
+
+            for n in range(UNITS):
+                cols = slice(N_TILE * n, N_TILE * (n + 1))
+                bias_sum = sums.tile([P, N_TILE], F32, tag="acc")
+                nc.tensor.matmul(out=bias_sum[:], lhsT=ones[:], rhs=bias_rows[:, cols], start=True, stop=True)
+                if n % 2 == 0:
+                    nc.scalar.copy(out=bias[:, cols], in_=bias_sum[:])
+                else:
+                    nc.vector.tensor_copy(out=bias[:, cols], in_=bias_sum[:])
+
+        gate_pool = ctx.enter_context(tc.tile_pool(name="gates", bufs=CHUNKS))
+
+        def transpose_and_quantise(unit):
+            rows_words = raw[unit][:].bitcast(F32)
+            codes = codes_pool.tile([P, H_PASSES, N_TILE], U32, tag="codes", align_bytes=64)
+            scales = codes_pool.tile([P, H_PASSES, N_TILE], U8, tag="scales", align_bytes=64)
+            grouped = []
+
+            def quantise(s):
+                nc.vector.quantize_mx(out=codes[:, s, :].bitcast(FP8X4), scales=scales[:, s, :], in_=grouped[s][:])
+
+            for s in range(H_PASSES):
+                group = grouped_pool.tile([P, PACK * N_TILE], BF16, tag="grouped", align_bytes=64)
+                grouped.append(group)
+                group_words = group[:].bitcast(F32).rearrange("p (q a w) -> p a q w", a=2, w=4)
+                on_vector = s == H_PASSES - 1 and unit % 2 == 1
+                for a in range(2):
+                    bank = transposed.tile([P, 4, P], F32, tag="bank")
+                    for w in range(4):
+                        first = WORDS_PASS * s + P * (w % 2)
+                        nc.tensor.transpose(
+                            out=bank[:, w, :], in_=rows_words[:, 2 * a + w // 2, first : first + P], identity=ident[:]
+                        )
+                    if on_vector:
+                        nc.vector.tensor_copy(out=group_words[:, a], in_=bank[:].rearrange("p w q -> p q w"))
+                    else:
+                        nc.scalar.copy(out=group_words[:, a], in_=bank[:].rearrange("p w q -> p q w"))
+                if s > 0:
+                    quantise(s - 1)
+            quantise(H_PASSES - 1)
+            wh_codes[unit] = (codes, scales)
+
+        for gate in range(GATES):
+            acc = []
+            for chunk in range(CHUNKS):
+                acc_tile = sums.tile([P, N_TILE], F32, tag="acc")
+                acc.append(acc_tile)
+            passes_done = [0] * CHUNKS
+
+            def next_flags(chunk):
+                passes_done[chunk] += 1
+                return passes_done[chunk] == 1, passes_done[chunk] == PASSES
+
+            def hidden_passes(chunk):
+                codes, scales = wh_codes[CHUNKS * gate + chunk]
+                for s in range(H_PASSES):
+                    start, stop = next_flags(chunk)
+                    nc.tensor.matmul_mx(
+                        out=acc[chunk][:],
+                        lhsT=h_codes[:, s, :].bitcast(FP8X4),
+                        lhsT_scale=h_scales[:, s, :],
+                        rhs=codes[:, s, :].bitcast(FP8X4),
+                        rhs_scale=scales[:, s, :],
+                        start=start,
+                        stop=stop,
+                    )
+
+            def input_passes():
+                for s in range(X_PASSES):
+                    for chunk in range(CHUNKS):
+                        start, stop = next_flags(chunk)
+                        nc.tensor.matmul_mx(
+                            out=acc[chunk][:],
+                            lhsT=x_codes[:, s, :].bitcast(FP8X4),
+                            lhsT_scale=x_scales[:, s, :],
+                            rhs=wx_words[gate][:, s, 2 * N_TILE * chunk : 2 * N_TILE * (chunk + 1)].bitcast(FP4X4),
+                            rhs_scale=wx_scales[:, X_PASSES * gate + s, N_TILE * chunk : N_TILE * (chunk + 1)],
+                            start=start,
+                            stop=stop,
+                        )
+
+            for chunk in range(CHUNKS):
+                unit = CHUNKS * gate + chunk
+                transpose_and_quantise(unit)
+                load_step(unit + LOOKAHEAD)
+                if chunk > 0:
+                    hidden_passes(chunk - 1)
+            input_passes()
+            hidden_passes(CHUNKS - 1)
+
+            values = []
+            for chunk in range(CHUNKS):
+                value = gate_pool.tile([P, N_TILE], F32, tag="gate%d" % gate)
+                first = HID * gate + N_TILE * chunk
+                nc.vector.tensor_add(out=value[:], in0=acc[chunk][:], in1=bias[:, first : first + N_TILE])
+                nc.scalar.activation(out=value[:], in_=value[:], func=GATE_FUNC[gate])
+                values.append(value)
+
+            if gate == 0:
+                in_gate = values
+            if gate == 1:
+                cell = values
+                for chunk in range(CHUNKS):
+                    cols = slice(N_TILE * chunk, N_TILE * (chunk + 1))
+                    nc.vector.tensor_mul(out=cell[chunk][:], in0=cell[chunk][:], in1=c_sb[:, cols])
+            if gate == 2:
+                cand = values
+                for chunk in range(CHUNKS):
+                    cols = slice(N_TILE * chunk, N_TILE * (chunk + 1))
+                    nc.vector.tensor_mul(out=in_gate[chunk][:], in0=in_gate[chunk][:], in1=cand[chunk][:])
+                    nc.vector.tensor_add(out=cell[chunk][:], in0=cell[chunk][:], in1=in_gate[chunk][:])
+                    nc.sync.dma_start(out=out_1[:, cols], in_=cell[chunk][:])
+                    nc.scalar.activation(out=cand[chunk][:], in_=cell[chunk][:], func=ACT.Tanh)
+            if gate == 3:
+                for chunk in range(CHUNKS):
+                    cols = slice(N_TILE * chunk, N_TILE * (chunk + 1))
+                    nc.vector.tensor_mul(out=values[chunk][:], in0=values[chunk][:], in1=cand[chunk][:])
+                    nc.sync.dma_start(out=out_0[:, cols], in_=values[chunk][:])

@@ -26,6 +26,7 @@ CHUNKS = HID // N_TILE
 UNITS = GATES * CHUNKS
 WORDS_PASS = K_PASS // 2
 ROWS_PART = N_TILE // P
+T_BANKS = 6
 LOOKAHEAD = 4
 GATE_FUNC = (ACT.Sigmoid, ACT.Sigmoid, ACT.Tanh, ACT.Sigmoid)
 
@@ -41,8 +42,8 @@ def tile_lstmcell_w_e_kernel(tc, x, h, c, Wx_words, Wx_scales, Wh, bx, bh, out_0
         words_pool = ctx.enter_context(tc.tile_pool(name="words", bufs=2))
         grouped_pool = ctx.enter_context(tc.tile_pool(name="grouped", bufs=2 * H_PASSES))
         codes_pool = ctx.enter_context(tc.tile_pool(name="codes", bufs=3))
-        transposed = ctx.enter_context(tc.psum_pool(name="transposed", bufs=5))
-        sums = ctx.enter_context(tc.psum_pool(name="sums", bufs=CHUNKS))
+        transposed = ctx.enter_context(tc.psum_pool(name="transposed", bufs=T_BANKS))
+        sums = ctx.enter_context(tc.psum_pool(name="sums", bufs=2))
 
         ident = const.tile([P, P], F32)
         make_identity(nc, ident[:])
@@ -77,10 +78,10 @@ def tile_lstmcell_w_e_kernel(tc, x, h, c, Wx_words, Wx_scales, Wh, bx, bh, out_0
             wx_words[gate] = words
 
         def load_step(n):
-            if n % CHUNKS == 0 and 0 < n <= UNITS:
-                load_input_weights(n // CHUNKS - 1)
             if n < UNITS:
                 load_hidden_weights(n)
+            if n % CHUNKS == 1 and n < UNITS:
+                load_input_weights(n // CHUNKS)
 
         def quantise_activation(src, passes, word_columns, grouped, codes, scales):
             src_words = src[:].bitcast(F32)
@@ -142,6 +143,9 @@ def tile_lstmcell_w_e_kernel(tc, x, h, c, Wx_words, Wx_scales, Wh, bx, bh, out_0
 
         gate_pool = ctx.enter_context(tc.tile_pool(name="gates", bufs=CHUNKS))
 
+        acc = {}
+        value = {}
+
         def transpose_and_quantise(unit):
             rows_words = raw[unit][:].bitcast(F32)
             codes = codes_pool.tile([P, H_PASSES, N_TILE], U32, tag="codes", align_bytes=64)
@@ -155,7 +159,6 @@ def tile_lstmcell_w_e_kernel(tc, x, h, c, Wx_words, Wx_scales, Wh, bx, bh, out_0
                 group = grouped_pool.tile([P, PACK * N_TILE], BF16, tag="grouped", align_bytes=64)
                 grouped.append(group)
                 group_words = group[:].bitcast(F32).rearrange("p (q a w) -> p a q w", a=2, w=4)
-                on_vector = s == H_PASSES - 1 and unit % 2 == 1
                 for a in range(2):
                     bank = transposed.tile([P, 4, P], F32, tag="bank")
                     for w in range(4):
@@ -163,7 +166,7 @@ def tile_lstmcell_w_e_kernel(tc, x, h, c, Wx_words, Wx_scales, Wh, bx, bh, out_0
                         nc.tensor.transpose(
                             out=bank[:, w, :], in_=rows_words[:, 2 * a + w // 2, first : first + P], identity=ident[:]
                         )
-                    if on_vector:
+                    if s == H_PASSES - 1 and a == 1:
                         nc.vector.tensor_copy(out=group_words[:, a], in_=bank[:].rearrange("p w q -> p q w"))
                     else:
                         nc.scalar.copy(out=group_words[:, a], in_=bank[:].rearrange("p w q -> p q w"))
@@ -172,79 +175,73 @@ def tile_lstmcell_w_e_kernel(tc, x, h, c, Wx_words, Wx_scales, Wh, bx, bh, out_0
             quantise(H_PASSES - 1)
             wh_codes[unit] = (codes, scales)
 
-        for gate in range(GATES):
-            acc = []
-            for chunk in range(CHUNKS):
-                acc_tile = sums.tile([P, N_TILE], F32, tag="acc")
-                acc.append(acc_tile)
-            passes_done = [0] * CHUNKS
+        def multiply(unit):
+            gate, chunk = divmod(unit, CHUNKS)
+            acc_tile = sums.tile([P, N_TILE], F32, tag="acc")
+            acc[unit] = acc_tile
+            codes, scales = wh_codes[unit]
+            for s in range(H_PASSES):
+                nc.tensor.matmul_mx(
+                    out=acc_tile[:],
+                    lhsT=h_codes[:, s, :].bitcast(FP8X4),
+                    lhsT_scale=h_scales[:, s, :],
+                    rhs=codes[:, s, :].bitcast(FP8X4),
+                    rhs_scale=scales[:, s, :],
+                    start=s == 0,
+                    stop=False,
+                )
+            for s in range(X_PASSES):
+                nc.tensor.matmul_mx(
+                    out=acc_tile[:],
+                    lhsT=x_codes[:, s, :].bitcast(FP8X4),
+                    lhsT_scale=x_scales[:, s, :],
+                    rhs=wx_words[gate][:, s, 2 * N_TILE * chunk : 2 * N_TILE * (chunk + 1)].bitcast(FP4X4),
+                    rhs_scale=wx_scales[:, X_PASSES * gate + s, N_TILE * chunk : N_TILE * (chunk + 1)],
+                    start=False,
+                    stop=s == X_PASSES - 1,
+                )
 
-            def next_flags(chunk):
-                passes_done[chunk] += 1
-                return passes_done[chunk] == 1, passes_done[chunk] == PASSES
+        def add_bias(unit):
+            gate = unit // CHUNKS
+            value_tile = gate_pool.tile([P, N_TILE], F32, tag="gate%d" % gate)
+            value[unit] = value_tile
+            nc.vector.tensor_add(
+                out=value_tile[:], in0=acc[unit][:], in1=bias[:, N_TILE * unit : N_TILE * (unit + 1)]
+            )
 
-            def hidden_passes(chunk):
-                codes, scales = wh_codes[CHUNKS * gate + chunk]
-                for s in range(H_PASSES):
-                    start, stop = next_flags(chunk)
-                    nc.tensor.matmul_mx(
-                        out=acc[chunk][:],
-                        lhsT=h_codes[:, s, :].bitcast(FP8X4),
-                        lhsT_scale=h_scales[:, s, :],
-                        rhs=codes[:, s, :].bitcast(FP8X4),
-                        rhs_scale=scales[:, s, :],
-                        start=start,
-                        stop=stop,
-                    )
+        def squash(unit):
+            nc.scalar.activation(out=value[unit][:], in_=value[unit][:], func=GATE_FUNC[unit // CHUNKS])
 
-            def input_passes():
-                for s in range(X_PASSES):
-                    for chunk in range(CHUNKS):
-                        start, stop = next_flags(chunk)
-                        nc.tensor.matmul_mx(
-                            out=acc[chunk][:],
-                            lhsT=x_codes[:, s, :].bitcast(FP8X4),
-                            lhsT_scale=x_scales[:, s, :],
-                            rhs=wx_words[gate][:, s, 2 * N_TILE * chunk : 2 * N_TILE * (chunk + 1)].bitcast(FP4X4),
-                            rhs_scale=wx_scales[:, X_PASSES * gate + s, N_TILE * chunk : N_TILE * (chunk + 1)],
-                            start=start,
-                            stop=stop,
-                        )
-
-            for chunk in range(CHUNKS):
-                unit = CHUNKS * gate + chunk
-                transpose_and_quantise(unit)
-                load_step(unit + LOOKAHEAD)
-                if chunk > 0:
-                    hidden_passes(chunk - 1)
-            input_passes()
-            hidden_passes(CHUNKS - 1)
-
-            values = []
-            for chunk in range(CHUNKS):
-                value = gate_pool.tile([P, N_TILE], F32, tag="gate%d" % gate)
-                first = HID * gate + N_TILE * chunk
-                nc.vector.tensor_add(out=value[:], in0=acc[chunk][:], in1=bias[:, first : first + N_TILE])
-                nc.scalar.activation(out=value[:], in_=value[:], func=GATE_FUNC[gate])
-                values.append(value)
-
-            if gate == 0:
-                in_gate = values
+        def cell_on_vector(unit):
+            gate, chunk = divmod(unit, CHUNKS)
+            cols = slice(N_TILE * chunk, N_TILE * (chunk + 1))
             if gate == 1:
-                cell = values
-                for chunk in range(CHUNKS):
-                    cols = slice(N_TILE * chunk, N_TILE * (chunk + 1))
-                    nc.vector.tensor_mul(out=cell[chunk][:], in0=cell[chunk][:], in1=c_sb[:, cols])
+                nc.vector.tensor_mul(out=value[unit][:], in0=value[unit][:], in1=c_sb[:, cols])
             if gate == 2:
-                cand = values
-                for chunk in range(CHUNKS):
-                    cols = slice(N_TILE * chunk, N_TILE * (chunk + 1))
-                    nc.vector.tensor_mul(out=in_gate[chunk][:], in0=in_gate[chunk][:], in1=cand[chunk][:])
-                    nc.vector.tensor_add(out=cell[chunk][:], in0=cell[chunk][:], in1=in_gate[chunk][:])
-                    nc.sync.dma_start(out=out_1[:, cols], in_=cell[chunk][:])
-                    nc.scalar.activation(out=cand[chunk][:], in_=cell[chunk][:], func=ACT.Tanh)
+                in_gate, cell = value[chunk], value[CHUNKS + chunk]
+                nc.vector.tensor_mul(out=in_gate[:], in0=in_gate[:], in1=value[unit][:])
+                nc.vector.tensor_add(out=cell[:], in0=cell[:], in1=in_gate[:])
+                nc.sync.dma_start(out=out_1[:, cols], in_=cell[:])
             if gate == 3:
-                for chunk in range(CHUNKS):
-                    cols = slice(N_TILE * chunk, N_TILE * (chunk + 1))
-                    nc.vector.tensor_mul(out=values[chunk][:], in0=values[chunk][:], in1=cand[chunk][:])
-                    nc.sync.dma_start(out=out_0[:, cols], in_=values[chunk][:])
+                nc.vector.tensor_mul(out=value[unit][:], in0=value[unit][:], in1=value[2 * CHUNKS + chunk][:])
+                nc.sync.dma_start(out=out_0[:, cols], in_=value[unit][:])
+
+        def cell_on_scalar(unit):
+            gate, chunk = divmod(unit, CHUNKS)
+            if gate == 2:
+                nc.scalar.activation(out=value[unit][:], in_=value[CHUNKS + chunk][:], func=ACT.Tanh)
+
+        for n in range(UNITS + 3):
+            if 0 <= n - 2 < UNITS:
+                add_bias(n - 2)
+            if 0 <= n - 3 < UNITS:
+                cell_on_vector(n - 3)
+            if n < UNITS:
+                transpose_and_quantise(n)
+            if 0 <= n - 2 < UNITS:
+                squash(n - 2)
+            if 0 <= n - 3 < UNITS:
+                cell_on_scalar(n - 3)
+            if 0 <= n - 1 < UNITS:
+                multiply(n - 1)
+            load_step(n + LOOKAHEAD)

@@ -77,11 +77,6 @@ def tile_lstmcell_w_e_kernel(tc, x, h, c, Wx_words, Wx_scales, Wh, bx, bh, out_0
                 nc.sync.dma_start(out=words[:, s, :].bitcast(I32), in_=Wx_words[X_PASSES * gate + s].bitcast(I32))
             wx_words[gate] = words
 
-        def load_step(n):
-            if n < UNITS:
-                load_hidden_weights(n)
-            if n % CHUNKS == 1 and n < UNITS:
-                load_input_weights(n // CHUNKS)
 
         def quantise_activation(src, passes, word_columns, grouped, codes, scales):
             src_words = src[:].bitcast(F32)
@@ -95,43 +90,67 @@ def tile_lstmcell_w_e_kernel(tc, x, h, c, Wx_words, Wx_scales, Wh, bx, bh, out_0
                 )
                 nc.vector.quantize_mx(out=codes[:, s, :].bitcast(FP8X4), scales=scales[:, s, :], in_=grouped[:, s, :])
 
-        with tc.tile_pool(name="head", bufs=1) as head:
-            bias_rows = head.tile([P, GATES * HID], BF16)
-            nc.vector.memset(bias_rows[:], 0.0)
-            for gate in range(GATES):
-                nc.vector.memset(wx_scales[:, X_PASSES * gate : X_PASSES * (gate + 1), :].bitcast(I32), 0)
+        head = ctx.enter_context(tc.tile_pool(name="head", bufs=1))
+        bias_rows = head.tile([P, GATES * HID], BF16)
+        nc.vector.memset(bias_rows[:], 0.0)
+        for gate in range(GATES):
+            nc.vector.memset(wx_scales[:, X_PASSES * gate : X_PASSES * (gate + 1), :].bitcast(I32), 0)
+        x_raw = head.tile([P, IN], BF16)
+        h_raw = head.tile([P, HID], BF16)
 
-            x_raw = head.tile([P, IN], BF16)
+        def load_activations(which):
             nc.sync.dma_start(out=x_raw[:], in_=x[:, :])
-            h_raw = head.tile([P, HID], BF16)
             nc.sync.dma_start(out=h_raw[:], in_=h[:, :])
+
+        def load_cell(which):
+            nc.sync.dma_start(out=c_sb[:], in_=c[:, :])
+
+        def load_biases(which):
             nc.sync.dma_start(out=bias_rows[0:1, :], in_=bx.rearrange("(o g) n -> o (g n)", o=1))
             nc.sync.dma_start(out=bias_rows[1:2, :], in_=bh.rearrange("(o g) n -> o (g n)", o=1))
 
-            for half in range(2):
-                groups = slice(8 * half, 8 * (half + 1))
-                for b in range(2):
-                    for r in range(4):
-                        nc.sync.dma_start(
-                            out=wx_scales[32 * b + r : P : 64, groups, :].bitcast(I32),
-                            in_=Wx_scales[groups, 4 * b + r : 16 : 8, :].rearrange("s q n -> q s n").bitcast(I32),
-                        )
+        def load_scales(half):
+            groups = slice(8 * half, 8 * (half + 1))
+            for b in range(2):
+                for r in range(4):
+                    nc.sync.dma_start(
+                        out=wx_scales[32 * b + r : P : 64, groups, :].bitcast(I32),
+                        in_=Wx_scales[groups, 4 * b + r : 16 : 8, :].rearrange("s q n -> q s n").bitcast(I32),
+                    )
 
-            for n in range(LOOKAHEAD):
-                load_step(n)
-            nc.sync.dma_start(out=c_sb[:], in_=c[:, :])
+        loaders = {
+            "xh": load_activations, "c": load_cell, "bias": load_biases, "scales": load_scales,
+            "wh": load_hidden_weights, "wx": load_input_weights,
+        }
+        stream = [("xh", 0), ("wh", 0), ("wh", 1), ("bias", 0), ("scales", 0), ("scales", 1), ("wx", 0)]
+        stream += [("wh", 2), ("wh", 3), ("c", 0)]
+        for n in range(4, UNITS):
+            stream.append(("wh", n))
+            if n % CHUNKS == 1:
+                stream.append(("wx", n // CHUNKS))
+        issued = [0]
 
-            x_grouped = head.tile([P, X_PASSES, PACK * P], BF16, align_bytes=64)
-            quantise_activation(
-                x_raw, X_PASSES, lambda s, u: slice(WORDS_PASS * s + u, WORDS_PASS * (s + 1), 2),
-                x_grouped, x_codes, x_scales,
-            )
-            h_grouped = head.tile([P, H_PASSES, PACK * P], BF16, align_bytes=64)
-            quantise_activation(
-                h_raw, H_PASSES, lambda s, u: slice(WORDS_PASS * s + P * u, WORDS_PASS * s + P * (u + 1)),
-                h_grouped, h_codes, h_scales,
-            )
+        def load_through(unit):
+            for kind, index in stream[issued[0] :]:
+                if kind == "wh" and index > unit:
+                    break
+                loaders[kind](index)
+                issued[0] += 1
 
+        load_through(LOOKAHEAD - 1)
+
+        x_grouped = head.tile([P, X_PASSES, PACK * P], BF16, align_bytes=64)
+        quantise_activation(
+            x_raw, X_PASSES, lambda s, u: slice(WORDS_PASS * s + u, WORDS_PASS * (s + 1), 2),
+            x_grouped, x_codes, x_scales,
+        )
+        h_grouped = head.tile([P, H_PASSES, PACK * P], BF16, align_bytes=64)
+        quantise_activation(
+            h_raw, H_PASSES, lambda s, u: slice(WORDS_PASS * s + P * u, WORDS_PASS * s + P * (u + 1)),
+            h_grouped, h_codes, h_scales,
+        )
+
+        def spread_biases():
             for n in range(UNITS):
                 cols = slice(N_TILE * n, N_TILE * (n + 1))
                 bias_sum = sums.tile([P, N_TILE], F32, tag="acc")
@@ -238,10 +257,12 @@ def tile_lstmcell_w_e_kernel(tc, x, h, c, Wx_words, Wx_scales, Wh, bx, bh, out_0
                 cell_on_vector(n - 3)
             if n < UNITS:
                 transpose_and_quantise(n)
+            if n == 1:
+                spread_biases()
             if 0 <= n - 2 < UNITS:
                 squash(n - 2)
             if 0 <= n - 3 < UNITS:
                 cell_on_scalar(n - 3)
             if 0 <= n - 1 < UNITS:
                 multiply(n - 1)
-            load_step(n + LOOKAHEAD)
+            load_through(n + LOOKAHEAD)

@@ -27,6 +27,7 @@ UNITS = GATES * CHUNKS
 WORDS_PASS = K_PASS // 2
 ROWS_PART = N_TILE // P
 T_BANKS = 6
+LAST_GATE = UNITS - CHUNKS
 LOOKAHEAD = 4
 GATE_FUNC = (ACT.Sigmoid, ACT.Sigmoid, ACT.Tanh, ACT.Sigmoid)
 
@@ -126,8 +127,9 @@ def tile_lstmcell_w_e_kernel(tc, x, h, c, Wx_words, Wx_scales, Wh, bx, bh, out_0
         stream += [("wh", 2), ("wh", 3), ("c", 0)]
         for n in range(4, UNITS):
             stream.append(("wh", n))
-            if n % CHUNKS == 1:
+            if n % CHUNKS == 1 and n < LAST_GATE:
                 stream.append(("wx", n // CHUNKS))
+        stream.append(("wx", GATES - 1))
         issued = [0]
 
         def load_through(unit):
@@ -194,31 +196,48 @@ def tile_lstmcell_w_e_kernel(tc, x, h, c, Wx_words, Wx_scales, Wh, bx, bh, out_0
             quantise(H_PASSES - 1)
             wh_codes[unit] = (codes, scales)
 
-        def multiply(unit):
-            gate, chunk = divmod(unit, CHUNKS)
-            acc_tile = sums.tile([P, N_TILE], F32, tag="acc")
-            acc[unit] = acc_tile
+        def hidden_passes(unit, start, stop):
             codes, scales = wh_codes[unit]
             for s in range(H_PASSES):
                 nc.tensor.matmul_mx(
-                    out=acc_tile[:],
+                    out=acc[unit][:],
                     lhsT=h_codes[:, s, :].bitcast(FP8X4),
                     lhsT_scale=h_scales[:, s, :],
                     rhs=codes[:, s, :].bitcast(FP8X4),
                     rhs_scale=scales[:, s, :],
-                    start=s == 0,
-                    stop=False,
+                    start=start and s == 0,
+                    stop=stop and s == H_PASSES - 1,
                 )
-            for s in range(X_PASSES):
-                nc.tensor.matmul_mx(
-                    out=acc_tile[:],
-                    lhsT=x_codes[:, s, :].bitcast(FP8X4),
-                    lhsT_scale=x_scales[:, s, :],
-                    rhs=wx_words[gate][:, s, 2 * N_TILE * chunk : 2 * N_TILE * (chunk + 1)].bitcast(FP4X4),
-                    rhs_scale=wx_scales[:, X_PASSES * gate + s, N_TILE * chunk : N_TILE * (chunk + 1)],
-                    start=False,
-                    stop=s == X_PASSES - 1,
-                )
+
+        def input_pass(unit, s, start, stop):
+            gate, chunk = divmod(unit, CHUNKS)
+            nc.tensor.matmul_mx(
+                out=acc[unit][:],
+                lhsT=x_codes[:, s, :].bitcast(FP8X4),
+                lhsT_scale=x_scales[:, s, :],
+                rhs=wx_words[gate][:, s, 2 * N_TILE * chunk : 2 * N_TILE * (chunk + 1)].bitcast(FP4X4),
+                rhs_scale=wx_scales[:, X_PASSES * gate + s, N_TILE * chunk : N_TILE * (chunk + 1)],
+                start=start,
+                stop=stop,
+            )
+
+        def multiply(unit):
+            if unit < UNITS - 1:
+                acc_tile = sums.tile([P, N_TILE], F32, tag="acc")
+                acc[unit] = acc_tile
+            if unit < LAST_GATE:
+                hidden_passes(unit, True, False)
+                for s in range(X_PASSES):
+                    input_pass(unit, s, False, s == X_PASSES - 1)
+            elif unit < UNITS - 1:
+                hidden_passes(unit, True, False)
+            else:
+                last_acc = transposed.tile([P, N_TILE], F32, tag="bank")
+                acc[unit] = last_acc
+                for s in range(X_PASSES):
+                    for other in range(LAST_GATE, UNITS):
+                        input_pass(other, s, other == unit and s == 0, other < unit and s == X_PASSES - 1)
+                hidden_passes(unit, False, True)
 
         def add_bias(unit):
             gate = unit // CHUNKS
@@ -250,19 +269,25 @@ def tile_lstmcell_w_e_kernel(tc, x, h, c, Wx_words, Wx_scales, Wh, bx, bh, out_0
             if gate == 2:
                 nc.scalar.activation(out=value[unit][:], in_=value[CHUNKS + chunk][:], func=ACT.Tanh)
 
-        for n in range(UNITS + 3):
-            if 0 <= n - 2 < UNITS:
+        for n in range(UNITS + 1):
+            if 0 <= n - 2 < LAST_GATE:
                 add_bias(n - 2)
-            if 0 <= n - 3 < UNITS:
+            if 0 <= n - 3 < LAST_GATE:
                 cell_on_vector(n - 3)
             if n < UNITS:
                 transpose_and_quantise(n)
             if n == 1:
                 spread_biases()
-            if 0 <= n - 2 < UNITS:
+            if 0 <= n - 2 < LAST_GATE:
                 squash(n - 2)
-            if 0 <= n - 3 < UNITS:
+            if 0 <= n - 3 < LAST_GATE:
                 cell_on_scalar(n - 3)
             if 0 <= n - 1 < UNITS:
                 multiply(n - 1)
             load_through(n + LOOKAHEAD)
+        for unit in range(LAST_GATE, UNITS + 1):
+            if unit < UNITS:
+                add_bias(unit)
+                squash(unit)
+            if unit > LAST_GATE:
+                cell_on_vector(unit - 1)

@@ -110,8 +110,9 @@ def tile_lstmcell_w_e_kernel(tc, x, h, c, Wx_words, Wx_scales, Wh, bx, bh, out_0
             nc.sync.dma_start(out=bias_rows[0:1, :], in_=bx.rearrange("(o g) n -> o (g n)", o=1))
             nc.sync.dma_start(out=bias_rows[1:2, :], in_=bh.rearrange("(o g) n -> o (g n)", o=1))
 
-        def load_scales(half):
-            groups = slice(8 * half, 8 * (half + 1))
+        def load_scales(gates):
+            first, last = gates
+            groups = slice(X_PASSES * first, X_PASSES * (last + 1))
             for b in range(2):
                 for r in range(4):
                     nc.sync.dma_start(
@@ -123,12 +124,13 @@ def tile_lstmcell_w_e_kernel(tc, x, h, c, Wx_words, Wx_scales, Wh, bx, bh, out_0
             "xh": load_activations, "c": load_cell, "bias": load_biases, "scales": load_scales,
             "wh": load_hidden_weights, "wx": load_input_weights,
         }
-        stream = [("xh", 0), ("wh", 0), ("wh", 1), ("bias", 0), ("scales", 0), ("scales", 1), ("wx", 0)]
+        stream = [("xh", 0), ("wh", 0), ("wh", 1), ("bias", 0), ("scales", (0, 0)), ("scales", (1, 2)), ("wx", 0)]
         stream += [("wh", 2), ("wh", 3), ("c", 0)]
         for n in range(4, UNITS):
             stream.append(("wh", n))
             if n % CHUNKS == 1 and n < LAST_GATE:
                 stream.append(("wx", n // CHUNKS))
+        stream.append(("scales", (GATES - 1, GATES - 1)))
         stream.append(("wx", GATES - 1))
         issued = [0]
 

@@ -55,7 +55,12 @@ def tile_lstmcell_w_e_kernel(tc, x, h, c, Wx_words, Wx_scales, Wh, bx, bh, out_0
         x_scales = const.tile([P, X_PASSES, P], U8, align_bytes=64)
         h_codes = const.tile([P, H_PASSES, P], U32, align_bytes=64)
         h_scales = const.tile([P, H_PASSES, P], U8, align_bytes=64)
-        wx_scales = const.tile([P, GATES * X_PASSES, HID], U8, align_bytes=64)
+        SCALE_RUNS = ((0, 0), (1, 2), (3, 3))
+        scale_tiles = {}
+        for first, last in SCALE_RUNS:
+            planes = const.tile([P, (last - first + 1) * X_PASSES, HID], U8, name="planes%d" % first, align_bytes=64)
+            for gate in range(first, last + 1):
+                scale_tiles[gate] = (planes, first)
         bias = const.tile([P, GATES * HID], F32)
         c_sb = const.tile([P, HID], BF16)
 
@@ -95,7 +100,8 @@ def tile_lstmcell_w_e_kernel(tc, x, h, c, Wx_words, Wx_scales, Wh, bx, bh, out_0
         bias_rows = head.tile([P, GATES * HID], BF16)
         nc.vector.memset(bias_rows[:], 0.0)
         for gate in range(GATES):
-            nc.vector.memset(wx_scales[:, X_PASSES * gate : X_PASSES * (gate + 1), :].bitcast(I32), 0)
+            planes, first = scale_tiles[gate]
+            nc.vector.memset(planes[:, X_PASSES * (gate - first) : X_PASSES * (gate - first + 1), :].bitcast(I32), 0)
         x_raw = head.tile([P, IN], BF16)
         h_raw = head.tile([P, HID], BF16)
 
@@ -113,10 +119,11 @@ def tile_lstmcell_w_e_kernel(tc, x, h, c, Wx_words, Wx_scales, Wh, bx, bh, out_0
         def load_scales(gates):
             first, last = gates
             groups = slice(X_PASSES * first, X_PASSES * (last + 1))
+            planes = scale_tiles[first][0]
             for b in range(2):
                 for r in range(4):
                     nc.sync.dma_start(
-                        out=wx_scales[32 * b + r : P : 64, groups, :].bitcast(I32),
+                        out=planes[32 * b + r : P : 64, :, :].bitcast(I32),
                         in_=Wx_scales[groups, 4 * b + r : 16 : 8, :].rearrange("s q n -> q s n").bitcast(I32),
                     )
 
@@ -213,12 +220,13 @@ def tile_lstmcell_w_e_kernel(tc, x, h, c, Wx_words, Wx_scales, Wh, bx, bh, out_0
 
         def input_pass(unit, s, start, stop):
             gate, chunk = divmod(unit, CHUNKS)
+            planes, first = scale_tiles[gate]
             nc.tensor.matmul_mx(
                 out=acc[unit][:],
                 lhsT=x_codes[:, s, :].bitcast(FP8X4),
                 lhsT_scale=x_scales[:, s, :],
                 rhs=wx_words[gate][:, s, 2 * N_TILE * chunk : 2 * N_TILE * (chunk + 1)].bitcast(FP4X4),
-                rhs_scale=wx_scales[:, X_PASSES * gate + s, N_TILE * chunk : N_TILE * (chunk + 1)],
+                rhs_scale=planes[:, X_PASSES * (gate - first) + s, N_TILE * chunk : N_TILE * (chunk + 1)],
                 start=start,
                 stop=stop,
             )

@@ -78,10 +78,11 @@ def tile_lstmcell_w_e_kernel(tc, x, h, c, Wx_words, Wx_scales, Wh, bx, bh, out_0
             raw[unit] = rows
 
         def load_input_weights(gate):
-            words = words_pool.tile([P, X_PASSES, 2 * HID], U8, tag="words", align_bytes=64)
+            wx_words[gate] = []
             for s in range(X_PASSES):
-                nc.sync.dma_start(out=words[:, s, :].bitcast(I32), in_=Wx_words[X_PASSES * gate + s].bitcast(I32))
-            wx_words[gate] = words
+                words = words_pool.tile([P, 2 * HID], U8, tag="words%d" % s, align_bytes=64)
+                nc.sync.dma_start(out=words[:].bitcast(I32), in_=Wx_words[X_PASSES * gate + s].bitcast(I32))
+                wx_words[gate].append(words)
 
 
         def quantise_activation(src, passes, word_columns, grouped, codes, scales):
@@ -225,7 +226,7 @@ def tile_lstmcell_w_e_kernel(tc, x, h, c, Wx_words, Wx_scales, Wh, bx, bh, out_0
                 out=acc[unit][:],
                 lhsT=x_codes[:, s, :].bitcast(FP8X4),
                 lhsT_scale=x_scales[:, s, :],
-                rhs=wx_words[gate][:, s, 2 * N_TILE * chunk : 2 * N_TILE * (chunk + 1)].bitcast(FP4X4),
+                rhs=wx_words[gate][s][:, 2 * N_TILE * chunk : 2 * N_TILE * (chunk + 1)].bitcast(FP4X4),
                 rhs_scale=planes[:, X_PASSES * (gate - first) + s, N_TILE * chunk : N_TILE * (chunk + 1)],
                 start=start,
                 stop=stop,

@@ -114,8 +114,8 @@ def tile_lstmcell_w_e_kernel(tc, x, h, c, Wx_words, Wx_scales, Wh, bx, bh, out_0
             nc.sync.dma_start(out=c_sb[:], in_=c[:, :])
 
         def load_biases(which):
-            nc.sync.dma_start(out=bias_rows[0:1, :], in_=bx.rearrange("(o g) n -> o (g n)", o=1))
-            nc.sync.dma_start(out=bias_rows[1:2, :], in_=bh.rearrange("(o g) n -> o (g n)", o=1))
+            nc.sync.dma_start(out=bias_rows[8:9, :], in_=bx.rearrange("(o g) n -> o (g n)", o=1))
+            nc.sync.dma_start(out=bias_rows[72:73, :], in_=bh.rearrange("(o g) n -> o (g n)", o=1))
 
         def load_scales(gates):
             first, last = gates
@@ -261,19 +261,23 @@ def tile_lstmcell_w_e_kernel(tc, x, h, c, Wx_words, Wx_scales, Wh, bx, bh, out_0
         def squash(unit):
             nc.scalar.activation(out=value[unit][:], in_=value[unit][:], func=GATE_FUNC[unit // CHUNKS])
 
-        def cell_on_vector(unit):
+        def cell_products(unit):
             gate, chunk = divmod(unit, CHUNKS)
             cols = slice(N_TILE * chunk, N_TILE * (chunk + 1))
             if gate == 1:
                 nc.vector.tensor_mul(out=value[unit][:], in0=value[unit][:], in1=c_sb[:, cols])
             if gate == 2:
-                in_gate, cell = value[chunk], value[CHUNKS + chunk]
-                nc.vector.tensor_mul(out=in_gate[:], in0=in_gate[:], in1=value[unit][:])
-                nc.vector.tensor_add(out=cell[:], in0=cell[:], in1=in_gate[:])
-                nc.sync.dma_start(out=out_1[:, cols], in_=cell[:])
+                nc.vector.tensor_mul(out=value[chunk][:], in0=value[chunk][:], in1=value[unit][:])
             if gate == 3:
                 nc.vector.tensor_mul(out=value[unit][:], in0=value[unit][:], in1=value[2 * CHUNKS + chunk][:])
                 nc.sync.dma_start(out=out_0[:, cols], in_=value[unit][:])
+
+        def cell_sum(unit):
+            gate, chunk = divmod(unit, CHUNKS)
+            if gate == 2:
+                cell = value[CHUNKS + chunk]
+                nc.vector.tensor_add(out=cell[:], in0=cell[:], in1=value[chunk][:])
+                nc.sync.dma_start(out=out_1[:, N_TILE * chunk : N_TILE * (chunk + 1)], in_=cell[:])
 
         def cell_on_scalar(unit):
             gate, chunk = divmod(unit, CHUNKS)
@@ -281,24 +285,26 @@ def tile_lstmcell_w_e_kernel(tc, x, h, c, Wx_words, Wx_scales, Wh, bx, bh, out_0
                 nc.scalar.activation(out=value[unit][:], in_=value[CHUNKS + chunk][:], func=ACT.Tanh)
 
         for n in range(UNITS + 1):
+            if 0 <= n - 3 < LAST_GATE:
+                cell_products(n - 3)
             if 0 <= n - 2 < LAST_GATE:
                 add_bias(n - 2)
             if 0 <= n - 3 < LAST_GATE:
-                cell_on_vector(n - 3)
+                cell_sum(n - 3)
             if n < UNITS:
                 transpose_and_quantise(n)
             if n == 1:
                 spread_biases()
             if 0 <= n - 2 < LAST_GATE:
                 squash(n - 2)
-            if 0 <= n - 3 < LAST_GATE:
-                cell_on_scalar(n - 3)
+            if n == UNITS - 1:
+                for unit in range(2 * CHUNKS, LAST_GATE):
+                    cell_on_scalar(unit)
             if 0 <= n - 1 < UNITS:
                 multiply(n - 1)
             load_through(n + LOOKAHEAD)
-        for unit in range(LAST_GATE, UNITS + 1):
-            if unit < UNITS:
-                add_bias(unit)
-                squash(unit)
-            if unit > LAST_GATE:
-                cell_on_vector(unit - 1)
+        for unit in range(LAST_GATE, UNITS):
+            add_bias(unit)
+            squash(unit)
+        for unit in range(LAST_GATE, UNITS):
+            cell_products(unit)

@@ -41,6 +41,7 @@ def tile_lstmcell_w_e_kernel(tc, x, h, c, Wx_words, Wx_scales, Wh, bx, bh, out_0
         const = ctx.enter_context(tc.tile_pool(name="const", bufs=1))
         raw_pool = ctx.enter_context(tc.tile_pool(name="raw", bufs=LOOKAHEAD))
         words_pool = ctx.enter_context(tc.tile_pool(name="words", bufs=2))
+        last_words_pool = ctx.enter_context(tc.tile_pool(name="last_words", bufs=1))
         grouped_pool = ctx.enter_context(tc.tile_pool(name="grouped", bufs=2 * H_PASSES))
         codes_pool = ctx.enter_context(tc.tile_pool(name="codes", bufs=3))
         transposed = ctx.enter_context(tc.psum_pool(name="transposed", bufs=T_BANKS))
@@ -78,11 +79,21 @@ def tile_lstmcell_w_e_kernel(tc, x, h, c, Wx_words, Wx_scales, Wh, bx, bh, out_0
             raw[unit] = rows
 
         def load_input_weights(gate):
-            wx_words[gate] = []
-            for s in range(X_PASSES):
-                words = words_pool.tile([P, 2 * HID], U8, tag="words%d" % s, align_bytes=64)
-                nc.sync.dma_start(out=words[:].bitcast(I32), in_=Wx_words[X_PASSES * gate + s].bitcast(I32))
-                wx_words[gate].append(words)
+            if gate < GATES - 1:
+                words = words_pool.tile([P, X_PASSES, 2 * HID], U8, tag="words", align_bytes=64)
+                nc.sync.dma_start(
+                    out=words[:].bitcast(I32),
+                    in_=Wx_words[X_PASSES * gate : X_PASSES * (gate + 1)].rearrange("s p n -> p s n").bitcast(I32),
+                )
+                wx_words[gate] = [(words, s) for s in range(X_PASSES)]
+            else:
+                wx_words[gate] = []
+                for s in range(X_PASSES):
+                    words = last_words_pool.tile([P, 1, 2 * HID], U8, tag="words%d" % s, align_bytes=64)
+                    nc.sync.dma_start(
+                        out=words[:, 0, :].bitcast(I32), in_=Wx_words[X_PASSES * gate + s].bitcast(I32)
+                    )
+                    wx_words[gate].append((words, 0))
 
 
         def quantise_activation(src, passes, word_columns, grouped, codes, scales):
@@ -222,11 +233,12 @@ def tile_lstmcell_w_e_kernel(tc, x, h, c, Wx_words, Wx_scales, Wh, bx, bh, out_0
         def input_pass(unit, s, start, stop):
             gate, chunk = divmod(unit, CHUNKS)
             planes, first = scale_tiles[gate]
+            words, index = wx_words[gate][s]
             nc.tensor.matmul_mx(
                 out=acc[unit][:],
                 lhsT=x_codes[:, s, :].bitcast(FP8X4),
                 lhsT_scale=x_scales[:, s, :],
-                rhs=wx_words[gate][s][:, 2 * N_TILE * chunk : 2 * N_TILE * (chunk + 1)].bitcast(FP4X4),
+                rhs=words[:, index, 2 * N_TILE * chunk : 2 * N_TILE * (chunk + 1)].bitcast(FP4X4),
                 rhs_scale=planes[:, X_PASSES * (gate - first) + s, N_TILE * chunk : N_TILE * (chunk + 1)],
                 start=start,
                 stop=stop,

@@ -208,7 +208,7 @@ def tile_lstmcell_w_e_kernel(tc, x, h, c, Wx_words, Wx_scales, Wh, bx, bh, out_0
                         nc.tensor.transpose(
                             out=bank[:, w, :], in_=rows_words[:, 2 * a + w // 2, first : first + P], identity=ident[:]
                         )
-                    if s == H_PASSES - 1 and a == 1:
+                    if s == H_PASSES - 1 and a == 1 and unit < UNITS - 1:
                         nc.vector.tensor_copy(out=group_words[:, a], in_=bank[:].rearrange("p w q -> p q w"))
                     else:
                         nc.scalar.copy(out=group_words[:, a], in_=bank[:].rearrange("p w q -> p q w"))
@@ -244,23 +244,37 @@ def tile_lstmcell_w_e_kernel(tc, x, h, c, Wx_words, Wx_scales, Wh, bx, bh, out_0
                 stop=stop,
             )
 
+        def new_accumulator(unit):
+            acc_tile = sums.tile([P, N_TILE], F32, tag="acc")
+            acc[unit] = acc_tile
+
         def multiply(unit):
-            if unit < UNITS - 1:
-                acc_tile = sums.tile([P, N_TILE], F32, tag="acc")
-                acc[unit] = acc_tile
-            if unit < LAST_GATE:
-                hidden_passes(unit, True, False)
-                for s in range(X_PASSES):
-                    input_pass(unit, s, False, s == X_PASSES - 1)
-            elif unit < UNITS - 1:
-                hidden_passes(unit, True, False)
-            else:
+            chunk = unit % CHUNKS
+            if unit == UNITS - 1:
                 last_acc = transposed.tile([P, N_TILE], F32, tag="bank")
                 acc[unit] = last_acc
                 for s in range(X_PASSES):
                     for other in range(LAST_GATE, UNITS):
                         input_pass(other, s, other == unit and s == 0, other < unit and s == X_PASSES - 1)
                 hidden_passes(unit, False, True)
+            elif unit >= LAST_GATE:
+                new_accumulator(unit)
+                hidden_passes(unit, True, False)
+            elif chunk == 0:
+                new_accumulator(unit)
+                new_accumulator(unit + 1)
+                hidden_passes(unit, True, False)
+                for s in range(X_PASSES):
+                    input_pass(unit, s, False, s == X_PASSES - 1)
+                for s in range(X_PASSES):
+                    input_pass(unit + 1, s, s == 0, False)
+            elif chunk == 1:
+                hidden_passes(unit, False, True)
+            else:
+                new_accumulator(unit)
+                hidden_passes(unit, True, False)
+                for s in range(X_PASSES):
+                    input_pass(unit, s, False, s == X_PASSES - 1)
 
         def add_bias(unit):
             gate = unit // CHUNKS

from contextlib import ExitStack

import concourse.mybir as mybir
from concourse.masks import make_identity

F32 = mybir.dt.float32
BF16 = mybir.dt.bfloat16
I32 = mybir.dt.int32
U32 = mybir.dt.uint32
U8 = mybir.dt.uint8
FP8X4 = mybir.dt.float8_e4m3fn_x4
FP4X4 = mybir.dt.float4_e2m1fn_x4
ACT = mybir.ActivationFunctionType

P = 128
PACK = 4
K_PASS = P * PACK
IN = 2048
HID = 1536
GATES = 4
X_PASSES = IN // K_PASS
H_PASSES = HID // K_PASS
PASSES = X_PASSES + H_PASSES
N_TILE = 512
CHUNKS = HID // N_TILE
UNITS = GATES * CHUNKS
WORDS_PASS = K_PASS // 2
ROWS_PART = N_TILE // P
T_BANKS = 6
LAST_GATE = UNITS - CHUNKS
LOOKAHEAD = 4
GATE_FUNC = (ACT.Sigmoid, ACT.Sigmoid, ACT.Tanh, ACT.Sigmoid)

FLOPS = 2 * P * GATES * HID * (IN + HID)


def tile_lstmcell_w_e_kernel(tc, x, h, c, Wx_words, Wx_scales, Wh, bx, bh, out_0, out_1):
    nc = tc.nc
    with ExitStack() as ctx:
        ctx.enter_context(tc.manual_schedule())
        const = ctx.enter_context(tc.tile_pool(name="const", bufs=1))
        raw_pool = ctx.enter_context(tc.tile_pool(name="raw", bufs=LOOKAHEAD))
        words_pool = ctx.enter_context(tc.tile_pool(name="words", bufs=2))
        last_words_pool = ctx.enter_context(tc.tile_pool(name="last_words", bufs=1))
        grouped_pool = ctx.enter_context(tc.tile_pool(name="grouped", bufs=2 * H_PASSES))
        codes_pool = ctx.enter_context(tc.tile_pool(name="codes", bufs=3))
        transposed = ctx.enter_context(tc.psum_pool(name="transposed", bufs=T_BANKS))
        sums = ctx.enter_context(tc.psum_pool(name="sums", bufs=2))

        ident = const.tile([P, P], F32)
        make_identity(nc, ident[:])
        ones = const.tile([P, P], BF16)
        nc.vector.memset(ones[:], 1.0)

        x_codes = const.tile([P, X_PASSES, P], U32, align_bytes=64)
        x_scales = const.tile([P, X_PASSES, P], U8, align_bytes=64)
        h_codes = const.tile([P, H_PASSES, P], U32, align_bytes=64)
        h_scales = const.tile([P, H_PASSES, P], U8, align_bytes=64)
        SCALE_RUNS = ((0, 0), (1, 2), (3, 3))
        scale_tiles = {}
        for first, last in SCALE_RUNS:
            planes = const.tile([P, (last - first + 1) * X_PASSES, HID], U8, name="planes%d" % first, align_bytes=64)
            for gate in range(first, last + 1):
                scale_tiles[gate] = (planes, first)
        bias = const.tile([P, GATES * HID], F32)
        c_sb = const.tile([P, HID], BF16)

        raw = {}
        wx_words = {}
        wh_codes = {}

        def load_hidden_weights(unit):
            gate, chunk = divmod(unit, CHUNKS)
            rows = raw_pool.tile([P, ROWS_PART, HID], BF16, tag="rows")
            nc.sync.dma_start(
                out=rows[:],
                in_=Wh[gate, N_TILE * chunk : N_TILE * (chunk + 1), :].rearrange("(q r) k -> q r k", r=ROWS_PART),
            )
            raw[unit] = rows

        def load_input_weights(gate):
            if gate < GATES - 1:
                words = words_pool.tile([P, X_PASSES, 2 * HID], U8, tag="words", align_bytes=64)
                nc.sync.dma_start(
                    out=words[:].bitcast(I32),
                    in_=Wx_words[X_PASSES * gate : X_PASSES * (gate + 1)].rearrange("s p n -> p s n").bitcast(I32),
                )
                wx_words[gate] = [(words, s) for s in range(X_PASSES)]
            else:
                wx_words[gate] = []
                for s in range(X_PASSES):
                    words = last_words_pool.tile([P, 1, 2 * HID], U8, tag="words%d" % s, align_bytes=64)
                    nc.sync.dma_start(
                        out=words[:, 0, :].bitcast(I32), in_=Wx_words[X_PASSES * gate + s].bitcast(I32)
                    )
                    wx_words[gate].append((words, 0))


        def quantise_activation(src, passes, word_columns, grouped, codes, scales):
            src_words = src[:].bitcast(F32)
            for s in range(passes):
                bank = transposed.tile([P, 2, P], F32, tag="bank")
                for u in range(2):
                    nc.tensor.transpose(out=bank[:, u, :], in_=src_words[:, word_columns(s, u)], identity=ident[:])
                nc.scalar.copy(
                    out=grouped[:, s, :].bitcast(F32).rearrange("p (b u) -> p b u", u=2),
                    in_=bank[:].rearrange("p u b -> p b u"),
                )
                nc.vector.quantize_mx(out=codes[:, s, :].bitcast(FP8X4), scales=scales[:, s, :], in_=grouped[:, s, :])

        head = ctx.enter_context(tc.tile_pool(name="head", bufs=1))
        bias_rows = head.tile([P, GATES * HID], BF16)
        nc.vector.memset(bias_rows[:], 0.0)
        for gate in range(GATES):
            planes, first = scale_tiles[gate]
            nc.vector.memset(planes[:, X_PASSES * (gate - first) : X_PASSES * (gate - first + 1), :].bitcast(I32), 0)
        x_raw = head.tile([P, IN], BF16)
        h_raw = head.tile([P, HID], BF16)

        def load_activations(which):
            nc.sync.dma_start(out=x_raw[:], in_=x[:, :])
            nc.sync.dma_start(out=h_raw[:], in_=h[:, :])

        def load_cell(which):
            nc.sync.dma_start(out=c_sb[:], in_=c[:, :])

        def load_biases(which):
            nc.sync.dma_start(out=bias_rows[8:9, :], in_=bx.rearrange("(o g) n -> o (g n)", o=1))
            nc.sync.dma_start(out=bias_rows[72:73, :], in_=bh.rearrange("(o g) n -> o (g n)", o=1))

        def load_scales(gates):
            first, last = gates
            groups = slice(X_PASSES * first, X_PASSES * (last + 1))
            planes = scale_tiles[first][0]
            for b in range(2):
                for r in range(4):
                    nc.sync.dma_start(
                        out=planes[32 * b + r : P : 64, :, :].bitcast(I32),
                        in_=Wx_scales[groups, 4 * b + r : 16 : 8, :].rearrange("s q n -> q s n").bitcast(I32),
                    )

        loaders = {
            "xh": load_activations, "c": load_cell, "bias": load_biases, "scales": load_scales,
            "wh": load_hidden_weights, "wx": load_input_weights,
        }
        stream = [("xh", 0), ("wh", 0), ("wh", 1), ("bias", 0), ("scales", (0, 0)), ("scales", (1, 2)), ("wx", 0)]
        stream += [("wh", 2), ("wh", 3), ("c", 0)]
        for n in range(4, UNITS):
            stream.append(("wh", n))
            if n % CHUNKS == 1 and n < LAST_GATE:
                stream.append(("wx", n // CHUNKS))
        stream.append(("scales", (GATES - 1, GATES - 1)))
        stream.append(("wx", GATES - 1))
        issued = [0]

        def load_through(unit):
            for kind, index in stream[issued[0] :]:
                if kind == "wh" and index > unit:
                    break
                loaders[kind](index)
                issued[0] += 1

        load_through(LOOKAHEAD - 1)

        x_grouped = head.tile([P, X_PASSES, PACK * P], BF16, align_bytes=64)
        quantise_activation(
            x_raw, X_PASSES, lambda s, u: slice(WORDS_PASS * s + u, WORDS_PASS * (s + 1), 2),
            x_grouped, x_codes, x_scales,
        )
        h_grouped = head.tile([P, H_PASSES, PACK * P], BF16, align_bytes=64)
        quantise_activation(
            h_raw, H_PASSES, lambda s, u: slice(WORDS_PASS * s + P * u, WORDS_PASS * s + P * (u + 1)),
            h_grouped, h_codes, h_scales,
        )

        def spread_biases():
            for n in range(UNITS):
                cols = slice(N_TILE * n, N_TILE * (n + 1))
                bias_sum = sums.tile([P, N_TILE], F32, tag="acc")
                nc.tensor.matmul(out=bias_sum[:], lhsT=ones[:], rhs=bias_rows[:, cols], start=True, stop=True)
                if n % 2 == 0:
                    nc.scalar.copy(out=bias[:, cols], in_=bias_sum[:])
                else:
                    nc.vector.tensor_copy(out=bias[:, cols], in_=bias_sum[:])

        gate_pool = ctx.enter_context(tc.tile_pool(name="gates", bufs=CHUNKS))

        acc = {}
        value = {}

        def transpose_and_quantise(unit):
            rows_words = raw[unit][:].bitcast(F32)
            codes = codes_pool.tile([P, H_PASSES, N_TILE], U32, tag="codes", align_bytes=64)
            scales = codes_pool.tile([P, H_PASSES, N_TILE], U8, tag="scales", align_bytes=64)
            grouped = []

            def quantise(s):
                nc.vector.quantize_mx(out=codes[:, s, :].bitcast(FP8X4), scales=scales[:, s, :], in_=grouped[s][:])

            for s in range(H_PASSES):
                group = grouped_pool.tile([P, PACK * N_TILE], BF16, tag="grouped", align_bytes=64)
                grouped.append(group)
                group_words = group[:].bitcast(F32).rearrange("p (q a w) -> p a q w", a=2, w=4)
                for a in range(2):
                    bank = transposed.tile([P, 4, P], F32, tag="bank")
                    for w in range(4):
                        first = WORDS_PASS * s + P * (w % 2)
                        nc.tensor.transpose(
                            out=bank[:, w, :], in_=rows_words[:, 2 * a + w // 2, first : first + P], identity=ident[:]
                        )
                    if s == H_PASSES - 1 and a == 1 and unit < UNITS - 1:
                        nc.vector.tensor_copy(out=group_words[:, a], in_=bank[:].rearrange("p w q -> p q w"))
                    else:
                        nc.scalar.copy(out=group_words[:, a], in_=bank[:].rearrange("p w q -> p q w"))
                if s > 0:
                    quantise(s - 1)
            quantise(H_PASSES - 1)
            wh_codes[unit] = (codes, scales)

        def hidden_passes(unit, start, stop):
            codes, scales = wh_codes[unit]
            for s in range(H_PASSES):
                nc.tensor.matmul_mx(
                    out=acc[unit][:],
                    lhsT=h_codes[:, s, :].bitcast(FP8X4),
                    lhsT_scale=h_scales[:, s, :],
                    rhs=codes[:, s, :].bitcast(FP8X4),
                    rhs_scale=scales[:, s, :],
                    start=start and s == 0,
                    stop=stop and s == H_PASSES - 1,
                )

        def input_pass(unit, s, start, stop):
            gate, chunk = divmod(unit, CHUNKS)
            planes, first = scale_tiles[gate]
            words, index = wx_words[gate][s]
            nc.tensor.matmul_mx(
                out=acc[unit][:],
                lhsT=x_codes[:, s, :].bitcast(FP8X4),
                lhsT_scale=x_scales[:, s, :],
                rhs=words[:, index, 2 * N_TILE * chunk : 2 * N_TILE * (chunk + 1)].bitcast(FP4X4),
                rhs_scale=planes[:, X_PASSES * (gate - first) + s, N_TILE * chunk : N_TILE * (chunk + 1)],
                start=start,
                stop=stop,
            )

        def new_accumulator(unit):
            acc_tile = sums.tile([P, N_TILE], F32, tag="acc")
            acc[unit] = acc_tile

        def multiply(unit):
            chunk = unit % CHUNKS
            if unit == UNITS - 1:
                last_acc = transposed.tile([P, N_TILE], F32, tag="bank")
                acc[unit] = last_acc
                for s in range(X_PASSES):
                    for other in range(LAST_GATE, UNITS):
                        input_pass(other, s, other == unit and s == 0, other < unit and s == X_PASSES - 1)
                hidden_passes(unit, False, True)
            elif unit >= LAST_GATE:
                new_accumulator(unit)
                hidden_passes(unit, True, False)
            elif chunk == 0:
                new_accumulator(unit)
                new_accumulator(unit + 1)
                hidden_passes(unit, True, False)
                for s in range(X_PASSES):
                    input_pass(unit, s, False, s == X_PASSES - 1)
                for s in range(X_PASSES):
                    input_pass(unit + 1, s, s == 0, False)
            elif chunk == 1:
                hidden_passes(unit, False, True)
            else:
                new_accumulator(unit)
                hidden_passes(unit, True, False)
                for s in range(X_PASSES):
                    input_pass(unit, s, False, s == X_PASSES - 1)

        def add_bias(unit):
            gate = unit // CHUNKS
            value_tile = gate_pool.tile([P, N_TILE], F32, tag="gate%d" % gate)
            value[unit] = value_tile
            nc.vector.tensor_add(
                out=value_tile[:], in0=acc[unit][:], in1=bias[:, N_TILE * unit : N_TILE * (unit + 1)]
            )

        def squash(unit):
            nc.scalar.activation(out=value[unit][:], in_=value[unit][:], func=GATE_FUNC[unit // CHUNKS])

        def cell_products(unit):
            gate, chunk = divmod(unit, CHUNKS)
            cols = slice(N_TILE * chunk, N_TILE * (chunk + 1))
            if gate == 1:
                nc.vector.tensor_mul(out=value[unit][:], in0=value[unit][:], in1=c_sb[:, cols])
            if gate == 2:
                nc.vector.tensor_mul(out=value[chunk][:], in0=value[chunk][:], in1=value[unit][:])
            if gate == 3:
                nc.vector.tensor_mul(out=value[unit][:], in0=value[unit][:], in1=value[2 * CHUNKS + chunk][:])
                nc.sync.dma_start(out=out_0[:, cols], in_=value[unit][:])

        def cell_sum(unit):
            gate, chunk = divmod(unit, CHUNKS)
            if gate == 2:
                cell = value[CHUNKS + chunk]
                nc.vector.tensor_add(out=cell[:], in0=cell[:], in1=value[chunk][:])
                nc.sync.dma_start(out=out_1[:, N_TILE * chunk : N_TILE * (chunk + 1)], in_=cell[:])

        def cell_on_scalar(unit):
            gate, chunk = divmod(unit, CHUNKS)
            if gate == 2:
                nc.scalar.activation(out=value[unit][:], in_=value[CHUNKS + chunk][:], func=ACT.Tanh)

        for n in range(UNITS + 1):
            if 0 <= n - 3 < LAST_GATE:
                cell_products(n - 3)
            if 0 <= n - 2 < LAST_GATE:
                add_bias(n - 2)
            if 0 <= n - 3 < LAST_GATE:
                cell_sum(n - 3)
            if n < UNITS:
                transpose_and_quantise(n)
            if n == 1:
                spread_biases()
            if 0 <= n - 2 < LAST_GATE:
                squash(n - 2)
            if n == UNITS - 1:
                for unit in range(2 * CHUNKS, LAST_GATE):
                    cell_on_scalar(unit)
            if 0 <= n - 1 < UNITS:
                multiply(n - 1)
            load_through(n + LOOKAHEAD)
        for unit in range(LAST_GATE, UNITS):
            add_bias(unit)
            squash(unit)
        for unit in range(LAST_GATE, UNITS):
            cell_products(unit)
